import numpy as np
import ml_dtypes


def mxq(x, axis, fmt="e4m3"):
    dtype, down = {"e4m3": (ml_dtypes.float8_e4m3fn, 7), "e5m2": (ml_dtypes.float8_e5m2, 14)}[fmt]
    v = np.moveaxis(np.asarray(x, np.float32).astype(ml_dtypes.bfloat16).astype(np.float64), axis, -1)
    blocks = v.reshape(v.shape[:-1] + (-1, 32))
    amax = np.abs(blocks).max(-1, keepdims=True)
    byte = np.maximum(np.where(amax > 0, np.frexp(amax)[1] - 1 + 127, 0) - down, 1)
    scale = np.exp2(byte - 127.0)
    codes = (blocks / scale).astype(np.float32).astype(dtype).astype(np.float64)
    return np.moveaxis((codes * scale).reshape(v.shape), -1, axis)


WIDE = False


def mx_kscale(k):
    if not WIDE:
        return np.ones(k)
    levels = np.array([10, -10, 5, -5, 0])
    if k % 512:
        return np.exp2(np.random.permutation(np.resize(levels, k // 32))).repeat(32)
    a = np.empty((k // 512, 16))
    for p in range(k // 512):
        a[p, :8] = np.random.permutation(np.resize(levels, 8))
        for g in range(8):
            far = levels[np.abs(levels - a[p, g]) >= 10]
            a[p, g + 8] = far[np.random.randint(len(far))]
    return np.exp2(a.ravel()).repeat(32)


BF16 = ml_dtypes.bfloat16


def bf(x):
    return np.asarray(x, np.float32).astype(BF16)


def f64(x):
    return np.asarray(x).astype(np.float64)


E2M1 = np.array([0.0, 0.5, 1.0, 1.5, 2.0, 3.0, 4.0, 6.0, -0.0, -0.5, -1.0, -1.5, -2.0, -3.0, -4.0, -6.0])


def pack_weight(w, fmt):
    k, n = w.shape
    w = f64(bf(w)).reshape(k // 32, 32, n)
    amax = np.abs(w).max(1)
    if fmt == "e4m3":
        byte = np.frexp(amax)[1] - 1 + 127 - 7
    else:
        mant, ex = np.frexp(amax / 6.0)
        byte = np.where(mant > 0.5, ex, ex - 1) + 127
    byte = np.clip(np.where(amax > 0, byte, 1), 1, 254)
    scaled = (w * np.exp2(127.0 - byte)[:, None, :]).reshape(k, n).astype(np.float32)
    by_word = np.ascontiguousarray(scaled.reshape(k // 512, 128, 4, n).transpose(0, 1, 3, 2))
    if fmt == "e4m3":
        words = by_word.astype(ml_dtypes.float8_e4m3fn).view(np.uint8)
    else:
        c = by_word.astype(ml_dtypes.float4_e2m1fn).view(np.uint8) & 0xF
        words = c[..., 0::2] | (c[..., 1::2] << 4)
    return np.ascontiguousarray(words), np.ascontiguousarray(byte.astype(np.uint8).reshape(k // 512, 16, n))


def unpack_weight(words, scales, fmt):
    g, p, n, _ = words.shape
    if fmt == "e4m3":
        vals = np.ascontiguousarray(words).view(ml_dtypes.float8_e4m3fn).astype(np.float64)
    else:
        nib = np.empty((g, p, n, 4), np.uint8)
        nib[..., 0::2] = words & 0xF
        nib[..., 1::2] = words >> 4
        vals = E2M1[nib]
    vals = vals * np.repeat(np.exp2(scales.astype(np.float64) - 127.0), 8, axis=1)[..., None]
    return vals.transpose(0, 1, 3, 2).reshape(g * 512, n)


B, C, MID, HH, WW = 4, 256, 1024, 32, 32
N = HH * WW


def setup_inputs():
    s, t = mx_kscale(N), mx_kscale(MID)
    a = np.exp(1.5 * np.random.standard_normal((B, N, N)))
    a = a / a.sum(-1, keepdims=True)
    attn = bf(a * s)
    h_x = bf(np.random.standard_normal((B, MID, N)) * 2.0 * t[:, None] / s)
    v_w = np.random.standard_normal((C, MID)) * 3.0 / np.sqrt(MID) / t
    v_w_words, v_w_scales = pack_weight(np.ascontiguousarray(v_w.T), "e4m3")
    return {
        "attn": attn,
        "h_x": h_x,
        "v_w_words": v_w_words,
        "v_w_scales": v_w_scales,
        "v_b": bf(np.random.standard_normal(C) * 0.3),
        "x": bf(np.random.standard_normal((B, C, HH, WW))),
    }


def reference(attn, h_x, v_w_words, v_w_scales, v_b, x):
    z = mxq(f64(h_x), 2, "e4m3") @ mxq(f64(attn), 2, "e4m3").transpose(0, 2, 1)
    y = (unpack_weight(v_w_words, v_w_scales, "e4m3").T @ mxq(z, 1, "e4m3")) + f64(v_b)[None, :, None]
    return y.reshape(B, C, HH, WW) + f64(x)

@@ -1,0 +1,237 @@
+from contextlib import ExitStack
+
+import concourse.mybir as mybir
+from concourse.masks import make_identity
+
+BF16 = mybir.dt.bfloat16
+F32 = mybir.dt.float32
+I32 = mybir.dt.int32
+U32 = mybir.dt.uint32
+U8 = mybir.dt.uint8
+FP8X4 = mybir.dt.float8_e4m3fn_x4
+ADD = mybir.AluOpType.add
+
+BATCH = 4
+OUT_CH = 256
+MID_CH = 1024
+POS = 1024
+
+P = 128
+PACK = 4
+K_PASS = P * PACK
+PASSES = POS // K_PASS
+BANK = 512
+
+QUARTER = 512
+ROW_TILES = QUARTER // P
+QUARTERS = 4 * BATCH
+ROUNDS = 4 * BATCH
+Y_GROUPS = 4 * BATCH
+Y_COLS = POS // 4
+
+TRANSPOSE_AHEAD = 2
+LOAD_AHEAD = 6
+PROJECT_BEHIND = 2
+
+FLOPS = 2 * BATCH * (MID_CH * POS * POS + OUT_CH * MID_CH * POS)
+
+
+def tile_soablock_pb_t_kernel(tc, attn, h_x, v_w_words, v_w_scales, v_b, x, out):
+    nc = tc.nc
+    x_rows = x.rearrange("b c h w -> b c (h w)")
+    out_rows = out.rearrange("b c h w -> b c (h w)")
+
+    with ExitStack() as stack:
+        const = stack.enter_context(tc.tile_pool(name="const", bufs=1))
+        raw_pool = stack.enter_context(tc.tile_pool(name="raw", bufs=LOAD_AHEAD + 2))
+        grouped_pool = stack.enter_context(tc.tile_pool(name="grouped", bufs=2))
+        codes_pool = stack.enter_context(tc.tile_pool(name="codes", bufs=6))
+        z_grouped_pool = stack.enter_context(tc.tile_pool(name="z_grouped", bufs=2))
+        z_codes_pool = stack.enter_context(tc.tile_pool(name="z_codes", bufs=4))
+        x_pool = stack.enter_context(tc.tile_pool(name="x", bufs=3))
+        result_pool = stack.enter_context(tc.tile_pool(name="result", bufs=3))
+        z_psum = stack.enter_context(tc.psum_pool(name="z_psum", bufs=3))
+        wide_psum = stack.enter_context(tc.psum_pool(name="wide_psum", bufs=5))
+        stack.enter_context(tc.manual_schedule())
+
+        raws, groupeds, codes, planes = {}, {}, {}, {}
+        z_groupeds, z_codes, z_planes = {}, {}, {}
+        x_tiles, y_banks = {}, {}
+
+        def load_quarter(q):
+            b, half = q // 4, (q % 4) // 2
+            rows = slice(half * QUARTER, (half + 1) * QUARTER)
+            if q % 2 == 0:
+                source = h_x[b, rows, :].rearrange("(p j) m -> p j m", j=ROW_TILES)
+            else:
+                source = attn[b, rows, :].rearrange("(r p) m -> p r m", p=P)
+            raw = raw_pool.tile([P, ROW_TILES, POS], BF16)
+            for pair in range(ROW_TILES // 2):
+                two = slice(2 * pair, 2 * pair + 2)
+                nc.sync.dma_start(out=raw[:, two, :], in_=source[:, two, :])
+            raws[q] = raw
+            if q % 4 == 3:
+                x_tile = x_pool.tile([P, OUT_CH // P, POS], BF16)
+                nc.sync.dma_start(out=x_tile[:], in_=x_rows[b].rearrange("(t p) n -> p t n", p=P))
+                x_tiles[b] = x_tile
+
+        def transpose_quarter(q):
+            raw = raws[q]
+            grouped = grouped_pool.tile([P, PASSES, QUARTER, PACK], BF16, align_bytes=64)
+            for pair in range(ROW_TILES // 2):
+                for k in range(PASSES):
+                    bank = wide_psum.tile([P, BANK], F32, tag="wide")
+                    for u in range(2):
+                        for r in range(2):
+                            words = raw[:, 2 * pair + r, :].bitcast(F32)
+                            first = 2 * k * P + u
+                            nc.tensor.transpose(
+                                bank[:, (2 * u + r) * P : (2 * u + r + 1) * P],
+                                words[:, first : 2 * (k + 1) * P : 2],
+                                ident_f32[:],
+                            )
+                    rows = slice(2 * pair * P, (2 * pair + 2) * P)
+                    dest = grouped[:, k, rows, :].bitcast(F32)
+                    source = bank[:].rearrange("p (u r) -> p r u", u=2)
+                    if k == 0:
+                        nc.scalar.copy(out=dest, in_=source)
+                    else:
+                        nc.vector.tensor_copy(out=dest, in_=source)
+            groupeds[q] = grouped
+
+        def quantise_quarter(q):
+            grouped = groupeds[q]
+            code = codes_pool.tile([P, PASSES, QUARTER], U32, align_bytes=64)
+            plane = codes_pool.tile([P, PASSES, QUARTER], U8, align_bytes=64)
+            for k in range(PASSES):
+                nc.vector.quantize_mx(
+                    out=code[:, k, :].bitcast(FP8X4),
+                    scales=plane[:, k, :],
+                    in_=grouped[:, k, :, :].rearrange("p r t -> p (r t)"),
+                )
+            codes[q] = code
+            planes[q] = plane
+
+        def mix_round(i):
+            b, half, g = i // 4, (i % 4) // 2, i % 2
+            h_q, a_q = 4 * b + 2 * g, 4 * b + 2 * half + 1
+            z_grouped = z_grouped_pool.tile([P, QUARTER, PACK], BF16, align_bytes=64)
+            for chunk in range(QUARTER // P):
+                cols = slice(chunk * P, (chunk + 1) * P)
+                bank = z_psum.tile([P, PACK, P], F32)
+                for j in range(PACK):
+                    chans = slice(j * P, (j + 1) * P)
+                    for k in range(PASSES):
+                        nc.tensor.matmul_mx(
+                            out=bank[:, j, :],
+                            lhsT=codes[h_q][:, k, chans].bitcast(FP8X4),
+                            lhsT_scale=planes[h_q][:, k, chans],
+                            rhs=codes[a_q][:, k, cols].bitcast(FP8X4),
+                            rhs_scale=planes[a_q][:, k, cols],
+                            start=(k == 0),
+                            stop=(k == PASSES - 1),
+                        )
+                nc.scalar.copy(out=z_grouped[:, cols, :], in_=bank[:].rearrange("p j n -> p n j"))
+            z_groupeds[i] = z_grouped
+
+        def quantise_z(i, part):
+            if part == 0:
+                z_code = z_codes_pool.tile([P, QUARTER], U32, align_bytes=64)
+                z_plane = z_codes_pool.tile([P, QUARTER], U8, align_bytes=64)
+                z_codes[i] = z_code
+                z_planes[i] = z_plane
+            cols = slice(part * Y_COLS, (part + 1) * Y_COLS)
+            nc.vector.quantize_mx(
+                out=z_codes[i][:, cols].bitcast(FP8X4),
+                scales=z_planes[i][:, cols],
+                in_=z_groupeds[i][:, cols, :].rearrange("p n j -> p (n j)"),
+            )
+
+        def project(y):
+            b, half, part = y // 4, (y % 4) // 2, y % 2
+            cols = slice(part * Y_COLS, (part + 1) * Y_COLS)
+            bank = wide_psum.tile([P, BANK], F32, tag="wide")
+            for t in range(OUT_CH // P):
+                outs = slice(t * P, (t + 1) * P)
+                for g in range(PASSES):
+                    i = 4 * b + 2 * half + g
+                    nc.tensor.matmul_mx(
+                        out=bank[:, t * Y_COLS : (t + 1) * Y_COLS],
+                        lhsT=w_words[:, g, outs].bitcast(FP8X4),
+                        lhsT_scale=w_plane[:, g, outs],
+                        rhs=z_codes[i][:, cols].bitcast(FP8X4),
+                        rhs_scale=z_planes[i][:, cols],
+                        start=(g == 0),
+                        stop=(g == PASSES - 1),
+                    )
+            y_banks[y] = bank
+
+        def finish(y):
+            b = y // 4
+            cols = slice((y % 4) * Y_COLS, (y % 4 + 1) * Y_COLS)
+            result = result_pool.tile([P, OUT_CH // P, Y_COLS], F32)
+            for t in range(OUT_CH // P):
+                nc.vector.scalar_tensor_tensor(
+                    out=result[:, t, :],
+                    in0=y_banks[y][:, t * Y_COLS : (t + 1) * Y_COLS],
+                    scalar=bias[:, t : t + 1],
+                    in1=x_tiles[b][:, t, cols],
+                    op0=ADD,
+                    op1=ADD,
+                )
+            nc.sync.dma_start(
+                out=out_rows[b].rearrange("(t p) n -> p t n", p=P)[:, :, cols], in_=result[:]
+            )
+
+        ident_f32 = const.tile([P, P], F32)
+        make_identity(nc, ident_f32[:])
+        ident_bf16 = const.tile([P, P], BF16)
+        make_identity(nc, ident_bf16[:])
+
+        w_words = const.tile([P, PASSES, OUT_CH], U32, align_bytes=64)
+        w_plane = const.tile([P, PASSES, OUT_CH], U8, align_bytes=64)
+        nc.vector.memset(w_plane[:].bitcast(I32), 0)
+        bias_rows = const.tile([P, P], BF16)
+        nc.vector.memset(bias_rows[:], 0.0)
+
+        load_quarter(0)
+        load_quarter(1)
+        nc.sync.dma_start(out=bias_rows[0 : OUT_CH // P, :], in_=v_b.rearrange("(t p) -> t p", p=P))
+        load_quarter(2)
+        nc.sync.dma_start(
+            out=w_words[:].bitcast(I32),
+            in_=v_w_words.rearrange("g p o t -> p g (o t)").bitcast(I32),
+        )
+        for quad in range(4):
+            nc.sync.dma_start(
+                out=w_plane[32 * quad : 32 * quad + 4, :, :].bitcast(I32),
+                in_=v_w_scales[:, 4 * quad : 4 * quad + 4, :].rearrange("g r o -> r g o").bitcast(I32),
+            )
+        for q in range(3, LOAD_AHEAD):
+            load_quarter(q)
+
+        for q in range(TRANSPOSE_AHEAD):
+            transpose_quarter(q)
+            quantise_quarter(q)
+
+        bias_bank = wide_psum.tile([P, P], BF16, tag="wide")
+        nc.tensor.transpose(bias_bank[:], bias_rows[:], ident_bf16[:])
+        bias = const.tile([P, OUT_CH // P], F32)
+        nc.vector.tensor_copy(out=bias[:], in_=bias_bank[:, 0 : OUT_CH // P])
+
+        for i in range(ROUNDS + PROJECT_BEHIND + 1):
+            if i + LOAD_AHEAD < QUARTERS:
+                load_quarter(i + LOAD_AHEAD)
+            if 0 <= i - 1 < ROUNDS:
+                quantise_z(i - 1, 1)
+            if i + TRANSPOSE_AHEAD < QUARTERS:
+                transpose_quarter(i + TRANSPOSE_AHEAD)
+            if 0 <= i - PROJECT_BEHIND - 1 < Y_GROUPS:
+                finish(i - PROJECT_BEHIND - 1)
+            if i + TRANSPOSE_AHEAD < QUARTERS:
+                quantise_quarter(i + TRANSPOSE_AHEAD)
+            if i < ROUNDS:
+                mix_round(i)
+                quantise_z(i, 0)
+            if 0 <= i - PROJECT_BEHIND < Y_GROUPS:
+                project(i - PROJECT_BEHIND)

@@ -30,6 +30,7 @@ Y_GROUPS = 4 * BATCH
 Y_COLS = POS // 4
 
 TRANSPOSE_AHEAD = 2
+SORT_AHEAD = 3
 LOAD_AHEAD = 6
 PROJECT_BEHIND = 2
 
@@ -44,6 +45,7 @@ def tile_soablock_pb_t_kernel(tc, attn, h_x, v_w_words, v_w_scales, v_b, x, out)
     with ExitStack() as stack:
         const = stack.enter_context(tc.tile_pool(name="const", bufs=1))
         raw_pool = stack.enter_context(tc.tile_pool(name="raw", bufs=LOAD_AHEAD + 2))
+        sorted_pool = stack.enter_context(tc.tile_pool(name="sorted", bufs=3))
         grouped_pool = stack.enter_context(tc.tile_pool(name="grouped", bufs=2))
         codes_pool = stack.enter_context(tc.tile_pool(name="codes", bufs=6))
         z_grouped_pool = stack.enter_context(tc.tile_pool(name="z_grouped", bufs=2))
@@ -54,7 +56,7 @@ def tile_soablock_pb_t_kernel(tc, attn, h_x, v_w_words, v_w_scales, v_b, x, out)
         wide_psum = stack.enter_context(tc.psum_pool(name="wide_psum", bufs=5))
         stack.enter_context(tc.manual_schedule())
 
-        raws, groupeds, codes, planes = {}, {}, {}, {}
+        raws, sorteds, groupeds, codes, planes = {}, {}, {}, {}, {}
         z_groupeds, z_codes, z_planes = {}, {}, {}
         x_tiles, y_banks = {}, {}
 
@@ -75,28 +77,38 @@ def tile_soablock_pb_t_kernel(tc, attn, h_x, v_w_words, v_w_scales, v_b, x, out)
                 nc.sync.dma_start(out=x_tile[:], in_=x_rows[b].rearrange("(t p) n -> p t n", p=P))
                 x_tiles[b] = x_tile
 
-        def transpose_quarter(q):
+        def sort_quarter(q):
             raw = raws[q]
+            in_order = sorted_pool.tile([P, 2, ROW_TILES, POS // 2], BF16)
+            for pair in range(ROW_TILES // 2):
+                two = slice(2 * pair, 2 * pair + 2)
+                nc.vector.tensor_copy(
+                    out=in_order[:, :, two, :].rearrange("p u r (x s) -> p (r x) u s", s=16),
+                    in_=raw[:, two, :].rearrange("p r (x u s) -> p (r x) u s", u=2, s=16),
+                )
+            sorteds[q] = in_order
+
+        def transpose_quarter(q):
+            in_order = sorteds[q]
             grouped = grouped_pool.tile([P, PASSES, QUARTER, PACK], BF16, align_bytes=64)
             for pair in range(ROW_TILES // 2):
                 for k in range(PASSES):
                     bank = wide_psum.tile([P, BANK], F32, tag="wide")
                     for u in range(2):
                         for r in range(2):
-                            words = raw[:, 2 * pair + r, :].bitcast(F32)
-                            first = 2 * k * P + u
+                            words = in_order[:, u, 2 * pair + r, :].bitcast(F32)
                             nc.tensor.transpose(
                                 bank[:, (2 * u + r) * P : (2 * u + r + 1) * P],
-                                words[:, first : 2 * (k + 1) * P : 2],
+                                words[:, k * P : (k + 1) * P],
                                 ident_f32[:],
                             )
                     rows = slice(2 * pair * P, (2 * pair + 2) * P)
                     dest = grouped[:, k, rows, :].bitcast(F32)
                     source = bank[:].rearrange("p (u r) -> p r u", u=2)
-                    if k == 0:
-                        nc.scalar.copy(out=dest, in_=source)
-                    else:
+                    if pair == 0 and k == 1:
                         nc.vector.tensor_copy(out=dest, in_=source)
+                    else:
+                        nc.scalar.copy(out=dest, in_=source)
             groupeds[q] = grouped
 
         def quantise_quarter(q):
@@ -211,9 +223,11 @@ def tile_soablock_pb_t_kernel(tc, attn, h_x, v_w_words, v_w_scales, v_b, x, out)
             load_quarter(q)
 
         for q in range(TRANSPOSE_AHEAD):
+            sort_quarter(q)
             transpose_quarter(q)
             quantise_quarter(q)
 
+        sort_quarter(TRANSPOSE_AHEAD)
         bias_bank = wide_psum.tile([P, P], BF16, tag="wide")
         nc.tensor.transpose(bias_bank[:], bias_rows[:], ident_bf16[:])
         bias = const.tile([P, OUT_CH // P], F32)
@@ -228,6 +242,8 @@ def tile_soablock_pb_t_kernel(tc, attn, h_x, v_w_words, v_w_scales, v_b, x, out)
                 transpose_quarter(i + TRANSPOSE_AHEAD)
             if 0 <= i - PROJECT_BEHIND - 1 < Y_GROUPS:
                 finish(i - PROJECT_BEHIND - 1)
+            if i + SORT_AHEAD < QUARTERS:
+                sort_quarter(i + SORT_AHEAD)
             if i + TRANSPOSE_AHEAD < QUARTERS:
                 quantise_quarter(i + TRANSPOSE_AHEAD)
             if i < ROUNDS:

@@ -24,6 +24,8 @@ BANK = 512
 
 QUARTER = 512
 ROW_TILES = QUARTER // P
+PAIRS = ROW_TILES // 2
+PAIR_ROWS = 2 * P
 QUARTERS = 4 * BATCH
 ROUNDS = 4 * BATCH
 Y_GROUPS = 4 * BATCH
@@ -68,7 +70,7 @@ def tile_soablock_pb_t_kernel(tc, attn, h_x, v_w_words, v_w_scales, v_b, x, out)
             else:
                 source = attn[b, rows, :].rearrange("(r p) m -> p r m", p=P)
             raw = raw_pool.tile([P, ROW_TILES, POS], BF16)
-            for pair in range(ROW_TILES // 2):
+            for pair in range(PAIRS):
                 two = slice(2 * pair, 2 * pair + 2)
                 nc.sync.dma_start(out=raw[:, two, :], in_=source[:, two, :])
             raws[q] = raw
@@ -77,58 +79,67 @@ def tile_soablock_pb_t_kernel(tc, attn, h_x, v_w_words, v_w_scales, v_b, x, out)
                 nc.sync.dma_start(out=x_tile[:], in_=x_rows[b].rearrange("(t p) n -> p t n", p=P))
                 x_tiles[b] = x_tile
 
+        def sort_pair(q, pair):
+            if pair == 0:
+                in_order = sorted_pool.tile([P, 2, ROW_TILES, POS // 2], BF16)
+                sorteds[q] = in_order
+            two = slice(2 * pair, 2 * pair + 2)
+            nc.vector.tensor_copy(
+                out=sorteds[q][:, :, two, :].rearrange("p u r (x s) -> p (r x) u s", s=16),
+                in_=raws[q][:, two, :].rearrange("p r (x u s) -> p (r x) u s", u=2, s=16),
+            )
+
         def sort_quarter(q):
-            raw = raws[q]
-            in_order = sorted_pool.tile([P, 2, ROW_TILES, POS // 2], BF16)
-            for pair in range(ROW_TILES // 2):
-                two = slice(2 * pair, 2 * pair + 2)
-                nc.vector.tensor_copy(
-                    out=in_order[:, :, two, :].rearrange("p u r (x s) -> p (r x) u s", s=16),
-                    in_=raw[:, two, :].rearrange("p r (x u s) -> p (r x) u s", u=2, s=16),
-                )
-            sorteds[q] = in_order
+            for pair in range(PAIRS):
+                sort_pair(q, pair)
+
+        def transpose_pair(q, pair, vector_bank=None):
+            if pair == 0:
+                grouped = grouped_pool.tile([P, PASSES, QUARTER, PACK], BF16, align_bytes=64)
+                groupeds[q] = grouped
+            for k in range(PASSES):
+                bank = wide_psum.tile([P, BANK], F32, tag="wide")
+                for u in range(2):
+                    for r in range(2):
+                        words = sorteds[q][:, u, 2 * pair + r, :].bitcast(F32)
+                        nc.tensor.transpose(
+                            bank[:, (2 * u + r) * P : (2 * u + r + 1) * P],
+                            words[:, k * P : (k + 1) * P],
+                            ident_f32[:],
+                        )
+                rows = slice(2 * pair * P, (2 * pair + 2) * P)
+                dest = groupeds[q][:, k, rows, :].bitcast(F32)
+                source = bank[:].rearrange("p (u r) -> p r u", u=2)
+                if k == vector_bank:
+                    nc.vector.tensor_copy(out=dest, in_=source)
+                else:
+                    nc.scalar.copy(out=dest, in_=source)
 
         def transpose_quarter(q):
-            in_order = sorteds[q]
-            grouped = grouped_pool.tile([P, PASSES, QUARTER, PACK], BF16, align_bytes=64)
-            for pair in range(ROW_TILES // 2):
-                for k in range(PASSES):
-                    bank = wide_psum.tile([P, BANK], F32, tag="wide")
-                    for u in range(2):
-                        for r in range(2):
-                            words = in_order[:, u, 2 * pair + r, :].bitcast(F32)
-                            nc.tensor.transpose(
-                                bank[:, (2 * u + r) * P : (2 * u + r + 1) * P],
-                                words[:, k * P : (k + 1) * P],
-                                ident_f32[:],
-                            )
-                    rows = slice(2 * pair * P, (2 * pair + 2) * P)
-                    dest = grouped[:, k, rows, :].bitcast(F32)
-                    source = bank[:].rearrange("p (u r) -> p r u", u=2)
-                    if pair == 0 and k == 1:
-                        nc.vector.tensor_copy(out=dest, in_=source)
-                    else:
-                        nc.scalar.copy(out=dest, in_=source)
-            groupeds[q] = grouped
+            transpose_pair(q, 0, vector_bank=1)
+            transpose_pair(q, 1)
 
-        def quantise_quarter(q):
-            grouped = groupeds[q]
-            code = codes_pool.tile([P, PASSES, QUARTER], U32, align_bytes=64)
-            plane = codes_pool.tile([P, PASSES, QUARTER], U8, align_bytes=64)
+        def quantise_rows(q, first, count):
+            if first == 0:
+                code = codes_pool.tile([P, PASSES, QUARTER], U32, align_bytes=64)
+                plane = codes_pool.tile([P, PASSES, QUARTER], U8, align_bytes=64)
+                codes[q] = code
+                planes[q] = plane
+            rows = slice(first, first + count)
             for k in range(PASSES):
                 nc.vector.quantize_mx(
-                    out=code[:, k, :].bitcast(FP8X4),
-                    scales=plane[:, k, :],
-                    in_=grouped[:, k, :, :].rearrange("p r t -> p (r t)"),
+                    out=codes[q][:, k, rows].bitcast(FP8X4),
+                    scales=planes[q][:, k, rows],
+                    in_=groupeds[q][:, k, rows, :].rearrange("p r t -> p (r t)"),
                 )
-            codes[q] = code
-            planes[q] = plane
 
-        def mix_round(i):
+        def mix(i, chunks):
             b, half, g = i // 4, (i % 4) // 2, i % 2
             h_q, a_q = 4 * b + 2 * g, 4 * b + 2 * half + 1
-            z_grouped = z_grouped_pool.tile([P, QUARTER, PACK], BF16, align_bytes=64)
-            for chunk in range(QUARTER // P):
+            if chunks[0] == 0:
+                z_grouped = z_grouped_pool.tile([P, QUARTER, PACK], BF16, align_bytes=64)
+                z_groupeds[i] = z_grouped
+            for chunk in chunks:
                 cols = slice(chunk * P, (chunk + 1) * P)
                 bank = z_psum.tile([P, PACK, P], F32)
                 for j in range(PACK):
@@ -143,8 +154,7 @@ def tile_soablock_pb_t_kernel(tc, attn, h_x, v_w_words, v_w_scales, v_b, x, out)
                             start=(k == 0),
                             stop=(k == PASSES - 1),
                         )
-                nc.scalar.copy(out=z_grouped[:, cols, :], in_=bank[:].rearrange("p j n -> p n j"))
-            z_groupeds[i] = z_grouped
+                nc.scalar.copy(out=z_groupeds[i][:, cols, :], in_=bank[:].rearrange("p j n -> p n j"))
 
         def quantise_z(i, part):
             if part == 0:
@@ -206,10 +216,10 @@ def tile_soablock_pb_t_kernel(tc, attn, h_x, v_w_words, v_w_scales, v_b, x, out)
         bias_rows = const.tile([P, P], BF16)
         nc.vector.memset(bias_rows[:], 0.0)
 
-        load_quarter(0)
-        load_quarter(1)
+        for q in range(3):
+            load_quarter(q)
         nc.sync.dma_start(out=bias_rows[0 : OUT_CH // P, :], in_=v_b.rearrange("(t p) -> t p", p=P))
-        load_quarter(2)
+        load_quarter(3)
         nc.sync.dma_start(
             out=w_words[:].bitcast(I32),
             in_=v_w_words.rearrange("g p o t -> p g (o t)").bitcast(I32),
@@ -219,35 +229,50 @@ def tile_soablock_pb_t_kernel(tc, attn, h_x, v_w_words, v_w_scales, v_b, x, out)
                 out=w_plane[32 * quad : 32 * quad + 4, :, :].bitcast(I32),
                 in_=v_w_scales[:, 4 * quad : 4 * quad + 4, :].rearrange("g r o -> r g o").bitcast(I32),
             )
-        for q in range(3, LOAD_AHEAD):
+        for q in range(4, LOAD_AHEAD):
             load_quarter(q)
 
-        for q in range(TRANSPOSE_AHEAD):
-            sort_quarter(q)
-            transpose_quarter(q)
-            quantise_quarter(q)
-
-        sort_quarter(TRANSPOSE_AHEAD)
+        sort_pair(0, 0)
+        transpose_pair(0, 0)
+        sort_pair(0, 1)
+        transpose_pair(0, 1)
+        sort_pair(1, 0)
+        quantise_rows(0, 0, PAIR_ROWS)
+        transpose_pair(1, 0)
+        sort_pair(1, 1)
+        quantise_rows(0, PAIR_ROWS, PAIR_ROWS)
+        transpose_pair(1, 1)
+        quantise_rows(1, 0, PAIR_ROWS)
+        sort_pair(2, 0)
+        mix(0, (0, 1))
+        quantise_rows(1, PAIR_ROWS, PAIR_ROWS)
+        sort_pair(2, 1)
+        transpose_quarter(2)
+        sort_quarter(3)
+        quantise_rows(2, 0, QUARTER)
+        mix(0, (2, 3))
+        quantise_z(0, 0)
+        load_quarter(LOAD_AHEAD)
         bias_bank = wide_psum.tile([P, P], BF16, tag="wide")
         nc.tensor.transpose(bias_bank[:], bias_rows[:], ident_bf16[:])
         bias = const.tile([P, OUT_CH // P], F32)
         nc.vector.tensor_copy(out=bias[:], in_=bias_bank[:, 0 : OUT_CH // P])
 
-        for i in range(ROUNDS + PROJECT_BEHIND + 1):
+        for i in range(1, ROUNDS + PROJECT_BEHIND + 1):
             if i + LOAD_AHEAD < QUARTERS:
                 load_quarter(i + LOAD_AHEAD)
-            if 0 <= i - 1 < ROUNDS:
-                quantise_z(i - 1, 1)
-            if i + TRANSPOSE_AHEAD < QUARTERS:
-                transpose_quarter(i + TRANSPOSE_AHEAD)
             if 0 <= i - PROJECT_BEHIND - 1 < Y_GROUPS:
                 finish(i - PROJECT_BEHIND - 1)
+            if i + TRANSPOSE_AHEAD < QUARTERS:
+                transpose_quarter(i + TRANSPOSE_AHEAD)
+            if i - 1 < ROUNDS:
+                quantise_z(i - 1, 1)
             if i + SORT_AHEAD < QUARTERS:
                 sort_quarter(i + SORT_AHEAD)
             if i + TRANSPOSE_AHEAD < QUARTERS:
-                quantise_quarter(i + TRANSPOSE_AHEAD)
+                quantise_rows(i + TRANSPOSE_AHEAD, 0, QUARTER)
             if i < ROUNDS:
-                mix_round(i)
+                mix(i, range(QUARTER // P))
                 quantise_z(i, 0)
             if 0 <= i - PROJECT_BEHIND < Y_GROUPS:
                 project(i - PROJECT_BEHIND)

@@ -28,8 +28,6 @@ PAIRS = ROW_TILES // 2
 PAIR_ROWS = 2 * P
 QUARTERS = 4 * BATCH
 ROUNDS = 4 * BATCH
-Y_GROUPS = 4 * BATCH
-Y_COLS = POS // 4
 
 TRANSPOSE_AHEAD = 2
 SORT_AHEAD = 3
@@ -46,164 +44,201 @@ def tile_soablock_pb_t_kernel(tc, attn, h_x, v_w_words, v_w_scales, v_b, x, out)
 
     with ExitStack() as stack:
         const = stack.enter_context(tc.tile_pool(name="const", bufs=1))
-        raw_pool = stack.enter_context(tc.tile_pool(name="raw", bufs=LOAD_AHEAD + 2))
-        sorted_pool = stack.enter_context(tc.tile_pool(name="sorted", bufs=3))
+        raw_pool = stack.enter_context(tc.tile_pool(name="raw", bufs=PAIRS * (LOAD_AHEAD + 2)))
+        sorted_pool = stack.enter_context(tc.tile_pool(name="sorted", bufs=3 * PAIRS))
         grouped_pool = stack.enter_context(tc.tile_pool(name="grouped", bufs=2))
         codes_pool = stack.enter_context(tc.tile_pool(name="codes", bufs=6))
         z_grouped_pool = stack.enter_context(tc.tile_pool(name="z_grouped", bufs=2))
         z_codes_pool = stack.enter_context(tc.tile_pool(name="z_codes", bufs=4))
         x_pool = stack.enter_context(tc.tile_pool(name="x", bufs=3))
-        result_pool = stack.enter_context(tc.tile_pool(name="result", bufs=3))
+        result_pool = stack.enter_context(tc.tile_pool(name="result", bufs=6))
         z_psum = stack.enter_context(tc.psum_pool(name="z_psum", bufs=3))
         wide_psum = stack.enter_context(tc.psum_pool(name="wide_psum", bufs=5))
         stack.enter_context(tc.manual_schedule())
 
-        raws, sorteds, groupeds, codes, planes = {}, {}, {}, {}, {}
-        z_groupeds, z_codes, z_planes = {}, {}, {}
+        raws, sorteds, turned, groupeds, codes, planes = {}, {}, {}, {}, {}, {}
+        z_banks, z_groupeds, z_codes, z_planes = {}, {}, {}, {}
         x_tiles, y_banks = {}, {}
 
-        def load_quarter(q):
+        def load_pair(q, pair, step=2):
             b, half = q // 4, (q % 4) // 2
             rows = slice(half * QUARTER, (half + 1) * QUARTER)
             if q % 2 == 0:
                 source = h_x[b, rows, :].rearrange("(p j) m -> p j m", j=ROW_TILES)
             else:
                 source = attn[b, rows, :].rearrange("(r p) m -> p r m", p=P)
-            raw = raw_pool.tile([P, ROW_TILES, POS], BF16)
+            raw = raw_pool.tile([P, 2, POS], BF16)
+            for r in range(0, 2, step):
+                first = 2 * pair + r
+                nc.sync.dma_start(out=raw[:, r : r + step, :], in_=source[:, first : first + step, :])
+            raws[q, pair] = raw
+
+        def load_quarter(q):
             for pair in range(PAIRS):
-                two = slice(2 * pair, 2 * pair + 2)
-                nc.sync.dma_start(out=raw[:, two, :], in_=source[:, two, :])
-            raws[q] = raw
-            if q % 4 == 3:
-                x_tile = x_pool.tile([P, OUT_CH // P, POS], BF16)
-                nc.sync.dma_start(out=x_tile[:], in_=x_rows[b].rearrange("(t p) n -> p t n", p=P))
-                x_tiles[b] = x_tile
+                load_pair(q, pair)
+
+        def load_x(b):
+            x_tile = x_pool.tile([P, OUT_CH // P, POS], BF16)
+            nc.sync.dma_start(out=x_tile[:], in_=x_rows[b].rearrange("(t p) n -> p t n", p=P))
+            x_tiles[b] = x_tile
+
+        def words_as_loaded(q, pair):
+            words = raws[q, pair][:].bitcast(F32)
+            return words.rearrange("p r (w u) -> p r u w", u=2)
 
         def sort_pair(q, pair):
-            if pair == 0:
-                in_order = sorted_pool.tile([P, 2, ROW_TILES, POS // 2], BF16)
-                sorteds[q] = in_order
-            two = slice(2 * pair, 2 * pair + 2)
-            nc.vector.tensor_copy(
-                out=sorteds[q][:, :, two, :].rearrange("p u r (x s) -> p (r x) u s", s=16),
-                in_=raws[q][:, two, :].rearrange("p r (x u s) -> p (r x) u s", u=2, s=16),
-            )
+            in_order = sorted_pool.tile([P, 2, 2, POS // 4], F32)
+            nc.vector.tensor_copy(out=in_order[:], in_=words_as_loaded(q, pair))
+            sorteds[q, pair] = in_order
 
         def sort_quarter(q):
             for pair in range(PAIRS):
                 sort_pair(q, pair)
 
-        def transpose_pair(q, pair, vector_bank=None):
-            if pair == 0:
-                grouped = grouped_pool.tile([P, PASSES, QUARTER, PACK], BF16, align_bytes=64)
-                groupeds[q] = grouped
+        def transpose_pair(q, pair, words):
+            banks = []
             for k in range(PASSES):
-                bank = wide_psum.tile([P, BANK], F32, tag="wide")
-                for u in range(2):
-                    for r in range(2):
-                        words = sorteds[q][:, u, 2 * pair + r, :].bitcast(F32)
+                bank = wide_psum.tile([P, 2, PAIR_ROWS], F32, tag="wide")
+                banks.append(bank)
+            for r in range(2):
+                for k in range(PASSES):
+                    for u in range(2):
                         nc.tensor.transpose(
-                            bank[:, (2 * u + r) * P : (2 * u + r + 1) * P],
-                            words[:, k * P : (k + 1) * P],
+                            banks[k][:, u, r * P : (r + 1) * P],
+                            words[:, r, u, k * P : (k + 1) * P],
                             ident_f32[:],
                         )
-                rows = slice(2 * pair * P, (2 * pair + 2) * P)
-                dest = groupeds[q][:, k, rows, :].bitcast(F32)
-                source = bank[:].rearrange("p (u r) -> p r u", u=2)
-                if k == vector_bank:
-                    nc.vector.tensor_copy(out=dest, in_=source)
-                else:
-                    nc.scalar.copy(out=dest, in_=source)
+            turned[q, pair] = banks
+
+        def empty_turned(copy, q, pair, k):
+            if q not in groupeds:
+                grouped = grouped_pool.tile([P, PASSES, QUARTER, PACK], BF16, align_bytes=64)
+                groupeds[q] = grouped
+            rows = slice(pair * PAIR_ROWS, (pair + 1) * PAIR_ROWS)
+            copy(
+                out=groupeds[q][:, k, rows, :].bitcast(F32),
+                in_=turned[q, pair][k][:].rearrange("p u r -> p r u"),
+            )
 
         def transpose_quarter(q):
-            transpose_pair(q, 0, vector_bank=1)
-            transpose_pair(q, 1)
+            transpose_pair(q, 0, sorteds[q, 0][:])
+            empty_turned(nc.scalar.copy, q, 0, 0)
+            empty_turned(nc.vector.tensor_copy, q, 0, 1)
+            transpose_pair(q, 1, sorteds[q, 1][:])
+            empty_turned(nc.scalar.copy, q, 1, 0)
+            empty_turned(nc.scalar.copy, q, 1, 1)
 
-        def quantise_rows(q, first, count):
-            if first == 0:
+        def codes_of(q):
+            if q not in codes:
                 code = codes_pool.tile([P, PASSES, QUARTER], U32, align_bytes=64)
                 plane = codes_pool.tile([P, PASSES, QUARTER], U8, align_bytes=64)
                 codes[q] = code
                 planes[q] = plane
-            rows = slice(first, first + count)
+            return codes[q], planes[q]
+
+        def quantise_pair(q, pair):
+            code, plane = codes_of(q)
+            rows = slice(pair * PAIR_ROWS, (pair + 1) * PAIR_ROWS)
             for k in range(PASSES):
                 nc.vector.quantize_mx(
-                    out=codes[q][:, k, rows].bitcast(FP8X4),
-                    scales=planes[q][:, k, rows],
+                    out=code[:, k, rows].bitcast(FP8X4),
+                    scales=plane[:, k, rows],
                     in_=groupeds[q][:, k, rows, :].rearrange("p r t -> p (r t)"),
                 )
 
-        def mix(i, chunks):
+        def quantise_quarter(q):
+            code, plane = codes_of(q)
+            nc.vector.quantize_mx(
+                out=code[:].rearrange("p k r -> p (k r)").bitcast(FP8X4),
+                scales=plane[:].rearrange("p k r -> p (k r)"),
+                in_=groupeds[q][:].rearrange("p k r t -> p (k r t)"),
+            )
+
+        def mix(i, chunk, js):
             b, half, g = i // 4, (i % 4) // 2, i % 2
             h_q, a_q = 4 * b + 2 * g, 4 * b + 2 * half + 1
-            if chunks[0] == 0:
+            cols = slice(chunk * P, (chunk + 1) * P)
+            if js[0] == 0:
+                z_bank = z_psum.tile([P, PACK, P], F32)
+                z_banks[i, chunk] = z_bank
+            for j in js:
+                chans = slice(j * P, (j + 1) * P)
+                for k in range(PASSES):
+                    nc.tensor.matmul_mx(
+                        out=z_banks[i, chunk][:, j, :],
+                        lhsT=codes[h_q][:, k, chans].bitcast(FP8X4),
+                        lhsT_scale=planes[h_q][:, k, chans],
+                        rhs=codes[a_q][:, k, cols].bitcast(FP8X4),
+                        rhs_scale=planes[a_q][:, k, cols],
+                        start=(k == 0),
+                        stop=(k == PASSES - 1),
+                    )
+
+        def empty_z(i, chunk):
+            if chunk == 0:
                 z_grouped = z_grouped_pool.tile([P, QUARTER, PACK], BF16, align_bytes=64)
                 z_groupeds[i] = z_grouped
-            for chunk in chunks:
-                cols = slice(chunk * P, (chunk + 1) * P)
-                bank = z_psum.tile([P, PACK, P], F32)
-                for j in range(PACK):
-                    chans = slice(j * P, (j + 1) * P)
-                    for k in range(PASSES):
-                        nc.tensor.matmul_mx(
-                            out=bank[:, j, :],
-                            lhsT=codes[h_q][:, k, chans].bitcast(FP8X4),
-                            lhsT_scale=planes[h_q][:, k, chans],
-                            rhs=codes[a_q][:, k, cols].bitcast(FP8X4),
-                            rhs_scale=planes[a_q][:, k, cols],
-                            start=(k == 0),
-                            stop=(k == PASSES - 1),
-                        )
-                nc.scalar.copy(out=z_groupeds[i][:, cols, :], in_=bank[:].rearrange("p j n -> p n j"))
+            cols = slice(chunk * P, (chunk + 1) * P)
+            nc.scalar.copy(out=z_groupeds[i][:, cols, :], in_=z_banks[i, chunk][:].rearrange("p j n -> p n j"))
 
-        def quantise_z(i, part):
-            if part == 0:
+        def mix_chunks(i, chunks):
+            for chunk in chunks:
+                mix(i, chunk, range(PACK))
+                empty_z(i, chunk)
+
+        def quantise_z(i, first, count):
+            if first == 0:
                 z_code = z_codes_pool.tile([P, QUARTER], U32, align_bytes=64)
                 z_plane = z_codes_pool.tile([P, QUARTER], U8, align_bytes=64)
                 z_codes[i] = z_code
                 z_planes[i] = z_plane
-            cols = slice(part * Y_COLS, (part + 1) * Y_COLS)
+            cols = slice(first, first + count)
             nc.vector.quantize_mx(
                 out=z_codes[i][:, cols].bitcast(FP8X4),
                 scales=z_planes[i][:, cols],
                 in_=z_groupeds[i][:, cols, :].rearrange("p n j -> p (n j)"),
             )
 
-        def project(y):
-            b, half, part = y // 4, (y % 4) // 2, y % 2
-            cols = slice(part * Y_COLS, (part + 1) * Y_COLS)
+        def project(group):
+            b, half, tiles, first, count = group
             bank = wide_psum.tile([P, BANK], F32, tag="wide")
-            for t in range(OUT_CH // P):
+            for place, t in enumerate(tiles):
                 outs = slice(t * P, (t + 1) * P)
                 for g in range(PASSES):
                     i = 4 * b + 2 * half + g
                     nc.tensor.matmul_mx(
-                        out=bank[:, t * Y_COLS : (t + 1) * Y_COLS],
+                        out=bank[:, place * count : (place + 1) * count],
                         lhsT=w_words[:, g, outs].bitcast(FP8X4),
                         lhsT_scale=w_plane[:, g, outs],
-                        rhs=z_codes[i][:, cols].bitcast(FP8X4),
-                        rhs_scale=z_planes[i][:, cols],
+                        rhs=z_codes[i][:, first : first + count].bitcast(FP8X4),
+                        rhs_scale=z_planes[i][:, first : first + count],
                         start=(g == 0),
                         stop=(g == PASSES - 1),
                     )
-            y_banks[y] = bank
+            y_banks[group] = bank
 
-        def finish(y):
-            b = y // 4
-            cols = slice((y % 4) * Y_COLS, (y % 4 + 1) * Y_COLS)
-            result = result_pool.tile([P, OUT_CH // P, Y_COLS], F32)
-            for t in range(OUT_CH // P):
+        def finish(group):
+            b, half, tiles, first, count = group
+            cols = slice(half * QUARTER + first, half * QUARTER + first + count)
+            result = result_pool.tile([P, BANK], F32)
+            for place, t in enumerate(tiles):
+                part = slice(place * count, (place + 1) * count)
                 nc.vector.scalar_tensor_tensor(
-                    out=result[:, t, :],
-                    in0=y_banks[y][:, t * Y_COLS : (t + 1) * Y_COLS],
+                    out=result[:, part],
+                    in0=y_banks[group][:, part],
                     scalar=bias[:, t : t + 1],
                     in1=x_tiles[b][:, t, cols],
                     op0=ADD,
                     op1=ADD,
                 )
             nc.sync.dma_start(
-                out=out_rows[b].rearrange("(t p) n -> p t n", p=P)[:, :, cols], in_=result[:]
+                out=out_rows[b].rearrange("(t p) n -> p t n", p=P)[:, tiles[0] : tiles[-1] + 1, cols],
+                in_=result[:, 0 : len(tiles) * count].rearrange("p (t n) -> p t n", t=len(tiles)),
             )
+
+        groups = [(n // 4, (n % 4) // 2, (n % 2,), 0, QUARTER) for n in range(4 * BATCH - 2)]
+        both = tuple(range(OUT_CH // P))
+        last_groups = [(BATCH - 1, 1, both, 0, 2 * P), (BATCH - 1, 1, both, 2 * P, P), (BATCH - 1, 1, both, 3 * P, P)]
 
         ident_f32 = const.tile([P, P], F32)
         make_identity(nc, ident_f32[:])
@@ -216,8 +251,11 @@ def tile_soablock_pb_t_kernel(tc, attn, h_x, v_w_words, v_w_scales, v_b, x, out)
         bias_rows = const.tile([P, P], BF16)
         nc.vector.memset(bias_rows[:], 0.0)
 
-        for q in range(3):
-            load_quarter(q)
+        load_pair(1, 0, step=1)
+        load_pair(0, 0, step=1)
+        load_pair(0, 1, step=1)
+        load_pair(1, 1, step=1)
+        load_quarter(2)
         nc.sync.dma_start(out=bias_rows[0 : OUT_CH // P, :], in_=v_b.rearrange("(t p) -> t p", p=P))
         load_quarter(3)
         nc.sync.dma_start(
@@ -229,50 +267,68 @@ def tile_soablock_pb_t_kernel(tc, attn, h_x, v_w_words, v_w_scales, v_b, x, out)
                 out=w_plane[32 * quad : 32 * quad + 4, :, :].bitcast(I32),
                 in_=v_w_scales[:, 4 * quad : 4 * quad + 4, :].rearrange("g r o -> r g o").bitcast(I32),
             )
-        for q in range(4, LOAD_AHEAD):
+        load_x(0)
+        for q in range(4, LOAD_AHEAD + 1):
             load_quarter(q)
 
-        sort_pair(0, 0)
-        transpose_pair(0, 0)
-        sort_pair(0, 1)
-        transpose_pair(0, 1)
-        sort_pair(1, 0)
-        quantise_rows(0, 0, PAIR_ROWS)
-        transpose_pair(1, 0)
-        sort_pair(1, 1)
-        quantise_rows(0, PAIR_ROWS, PAIR_ROWS)
-        transpose_pair(1, 1)
-        quantise_rows(1, 0, PAIR_ROWS)
+        transpose_pair(1, 0, words_as_loaded(1, 0))
+        empty_turned(nc.scalar.copy, 1, 0, 0)
+        empty_turned(nc.scalar.copy, 1, 0, 1)
+        quantise_pair(1, 0)
+        transpose_pair(0, 0, words_as_loaded(0, 0))
+        empty_turned(nc.scalar.copy, 0, 0, 0)
+        empty_turned(nc.vector.tensor_copy, 0, 0, 1)
+        quantise_pair(0, 0)
+        transpose_pair(0, 1, words_as_loaded(0, 1))
+        empty_turned(nc.scalar.copy, 0, 1, 0)
+        empty_turned(nc.scalar.copy, 0, 1, 1)
+        quantise_pair(0, 1)
+        transpose_pair(1, 1, words_as_loaded(1, 1))
+        empty_turned(nc.scalar.copy, 1, 1, 0)
         sort_pair(2, 0)
-        mix(0, (0, 1))
-        quantise_rows(1, PAIR_ROWS, PAIR_ROWS)
+        empty_turned(nc.vector.tensor_copy, 1, 1, 1)
+        mix_chunks(0, (0, 1))
         sort_pair(2, 1)
+        quantise_pair(1, 1)
         transpose_quarter(2)
         sort_quarter(3)
-        quantise_rows(2, 0, QUARTER)
-        mix(0, (2, 3))
-        quantise_z(0, 0)
-        load_quarter(LOAD_AHEAD)
+        mix_chunks(0, (2, 3))
+        quantise_quarter(2)
         bias_bank = wide_psum.tile([P, P], BF16, tag="wide")
         nc.tensor.transpose(bias_bank[:], bias_rows[:], ident_bf16[:])
         bias = const.tile([P, OUT_CH // P], F32)
         nc.vector.tensor_copy(out=bias[:], in_=bias_bank[:, 0 : OUT_CH // P])
 
-        for i in range(1, ROUNDS + PROJECT_BEHIND + 1):
+        for i in range(1, ROUNDS - 1):
             if i + LOAD_AHEAD < QUARTERS:
                 load_quarter(i + LOAD_AHEAD)
-            if 0 <= i - PROJECT_BEHIND - 1 < Y_GROUPS:
-                finish(i - PROJECT_BEHIND - 1)
+                if (i + LOAD_AHEAD) % 4 == 3:
+                    load_x((i + LOAD_AHEAD) // 4)
+            if i - PROJECT_BEHIND - 1 >= 0:
+                finish(groups[i - PROJECT_BEHIND - 1])
             if i + TRANSPOSE_AHEAD < QUARTERS:
                 transpose_quarter(i + TRANSPOSE_AHEAD)
-            if i - 1 < ROUNDS:
-                quantise_z(i - 1, 1)
+            quantise_z(i - 1, 0, QUARTER)
             if i + SORT_AHEAD < QUARTERS:
                 sort_quarter(i + SORT_AHEAD)
             if i + TRANSPOSE_AHEAD < QUARTERS:
-                quantise_rows(i + TRANSPOSE_AHEAD, 0, QUARTER)
-            if i < ROUNDS:
-                mix(i, range(QUARTER // P))
-                quantise_z(i, 0)
-            if 0 <= i - PROJECT_BEHIND < Y_GROUPS:
-                project(i - PROJECT_BEHIND)
+                quantise_quarter(i + TRANSPOSE_AHEAD)
+            mix_chunks(i, range(QUARTER // P))
+            if i - PROJECT_BEHIND >= 0:
+                project(groups[i - PROJECT_BEHIND])
+
+        i = ROUNDS - 1
+        finish(groups[-2])
+        quantise_z(i - 1, 0, QUARTER)
+        mix_chunks(i, (0, 1))
+        quantise_z(i, 0, 2 * P)
+        project(groups[-1])
+        mix_chunks(i, (2,))
+        quantise_z(i, 2 * P, P)
+        mix_chunks(i, (3,))
+        finish(groups[-1])
+        quantise_z(i, 3 * P, P)
+        for group in last_groups:
+            project(group)
+        for group in last_groups:
+            finish(group)

@@ -120,13 +120,12 @@ def tile_soablock_pb_t_kernel(tc, attn, h_x, v_w_words, v_w_scales, v_b, x, out)
                 in_=turned[q, pair][k][:].rearrange("p u r -> p r u"),
             )
 
-        def transpose_quarter(q):
-            transpose_pair(q, 0, sorteds[q, 0][:])
-            empty_turned(nc.scalar.copy, q, 0, 0)
-            empty_turned(nc.vector.tensor_copy, q, 0, 1)
-            transpose_pair(q, 1, sorteds[q, 1][:])
-            empty_turned(nc.scalar.copy, q, 1, 0)
-            empty_turned(nc.scalar.copy, q, 1, 1)
+        def transpose_quarter(q, vector_bank=2):
+            for pair in range(PAIRS):
+                transpose_pair(q, pair, sorteds[q, pair][:])
+                for k in range(PASSES):
+                    on_vector = PASSES * pair + k == vector_bank
+                    empty_turned(nc.vector.tensor_copy if on_vector else nc.scalar.copy, q, pair, k)
 
         def codes_of(q):
             if q not in codes:
@@ -290,7 +289,7 @@ def tile_soablock_pb_t_kernel(tc, attn, h_x, v_w_words, v_w_scales, v_b, x, out)
         mix_chunks(0, (0, 1))
         sort_pair(2, 1)
         quantise_pair(1, 1)
-        transpose_quarter(2)
+        transpose_quarter(2, vector_bank=1)
         sort_quarter(3)
         mix_chunks(0, (2, 3))
         quantise_quarter(2)

@@ -88,7 +88,10 @@ def tile_soablock_pb_t_kernel(tc, attn, h_x, v_w_words, v_w_scales, v_b, x, out)
 
         def sort_pair(q, pair):
             in_order = sorted_pool.tile([P, 2, 2, POS // 4], F32)
-            nc.vector.tensor_copy(out=in_order[:], in_=words_as_loaded(q, pair))
+            nc.vector.tensor_copy(
+                out=in_order[:].rearrange("p r u w -> p r w u"),
+                in_=raws[q, pair][:].bitcast(F32).rearrange("p r (w u) -> p r w u", u=2),
+            )
             sorteds[q, pair] = in_order
 
         def sort_quarter(q):
@@ -178,7 +181,10 @@ def tile_soablock_pb_t_kernel(tc, attn, h_x, v_w_words, v_w_scales, v_b, x, out)
                 z_grouped = z_grouped_pool.tile([P, QUARTER, PACK], BF16, align_bytes=64)
                 z_groupeds[i] = z_grouped
             cols = slice(chunk * P, (chunk + 1) * P)
-            nc.scalar.copy(out=z_groupeds[i][:, cols, :], in_=z_banks[i, chunk][:].rearrange("p j n -> p n j"))
+            nc.scalar.copy(
+                out=z_groupeds[i][:, cols, :].rearrange("p (c i) j -> p c j i", i=4),
+                in_=z_banks[i, chunk][:].rearrange("p j (c i) -> p c j i", i=4),
+            )
 
         def mix_chunks(i, chunks):
             for chunk in chunks:

@@ -32,6 +32,7 @@ ROUNDS = 4 * BATCH
 TRANSPOSE_AHEAD = 2
 SORT_AHEAD = 3
 LOAD_AHEAD = 6
+WORD_ORDER = 4
 PROJECT_BEHIND = 2
 
 FLOPS = 2 * BATCH * (MID_CH * POS * POS + OUT_CH * MID_CH * POS)
@@ -84,14 +85,17 @@ def tile_soablock_pb_t_kernel(tc, attn, h_x, v_w_words, v_w_scales, v_b, x, out)
 
         def words_as_loaded(q, pair):
             words = raws[q, pair][:].bitcast(F32)
-            return words.rearrange("p r (w u) -> p r u w", u=2)
+            return words.rearrange("p r (w u) -> p u r w", u=2)
 
         def sort_pair(q, pair):
-            in_order = sorted_pool.tile([P, 2, 2, POS // 4], F32)
-            nc.vector.tensor_copy(
-                out=in_order[:].rearrange("p r u w -> p r w u"),
-                in_=raws[q, pair][:].bitcast(F32).rearrange("p r (w u) -> p r w u", u=2),
-            )
+            in_order = sorted_pool.tile([P, 2, 2, POS // 2], BF16)
+            if q < WORD_ORDER:
+                nc.vector.tensor_copy(out=in_order[:].bitcast(F32), in_=words_as_loaded(q, pair))
+            else:
+                nc.vector.tensor_copy(
+                    out=in_order[:].rearrange("p u r (x s) -> p (r x) u s", s=16),
+                    in_=raws[q, pair][:].rearrange("p r (x u s) -> p (r x) u s", u=2, s=16),
+                )
             sorteds[q, pair] = in_order
 
         def sort_quarter(q):
@@ -108,7 +112,7 @@ def tile_soablock_pb_t_kernel(tc, attn, h_x, v_w_words, v_w_scales, v_b, x, out)
                     for u in range(2):
                         nc.tensor.transpose(
                             banks[k][:, u, r * P : (r + 1) * P],
-                            words[:, r, u, k * P : (k + 1) * P],
+                            words[:, u, r, k * P : (k + 1) * P],
                             ident_f32[:],
                         )
             turned[q, pair] = banks
@@ -125,7 +129,7 @@ def tile_soablock_pb_t_kernel(tc, attn, h_x, v_w_words, v_w_scales, v_b, x, out)
 
         def transpose_quarter(q, vector_bank=2):
             for pair in range(PAIRS):
-                transpose_pair(q, pair, sorteds[q, pair][:])
+                transpose_pair(q, pair, sorteds[q, pair][:].bitcast(F32))
                 for k in range(PASSES):
                     on_vector = PASSES * pair + k == vector_bank
                     empty_turned(nc.vector.tensor_copy if on_vector else nc.scalar.copy, q, pair, k)

@@ -131,7 +131,8 @@ def tile_soablock_pb_t_kernel(tc, attn, h_x, v_w_words, v_w_scales, v_b, x, out)
             for pair in range(PAIRS):
                 transpose_pair(q, pair, sorteds[q, pair][:].bitcast(F32))
                 for k in range(PASSES):
-                    on_vector = PASSES * pair + k == vector_bank
+                    number = PASSES * pair + k
+                    on_vector = number == vector_bank or (number == 0 and q >= WORD_ORDER and q % 2 == 0)
                     empty_turned(nc.vector.tensor_copy if on_vector else nc.scalar.copy, q, pair, k)
 
         def codes_of(q):
@@ -189,6 +190,30 @@ def tile_soablock_pb_t_kernel(tc, attn, h_x, v_w_words, v_w_scales, v_b, x, out)
                 out=z_groupeds[i][:, cols, :].rearrange("p (c i) j -> p c j i", i=4),
                 in_=z_banks[i, chunk][:].rearrange("p j (c i) -> p c j i", i=4),
             )
+
+        def mix_wide(i, chunks):
+            b, half, g = i // 4, (i % 4) // 2, i % 2
+            h_q, a_q = 4 * b + 2 * g, 4 * b + 2 * half + 1
+            cols = slice(chunks[0] * P, (chunks[0] + 2) * P)
+            if chunks[0] == 0:
+                z_grouped = z_grouped_pool.tile([P, QUARTER, PACK], BF16, align_bytes=64)
+                z_groupeds[i] = z_grouped
+            for jp in range(2):
+                z_bank = z_psum.tile([P, 2, 2 * P], F32)
+                for jj in range(2):
+                    j = 2 * jp + jj
+                    chans = slice(j * P, (j + 1) * P)
+                    for k in range(PASSES):
+                        nc.tensor.matmul_mx(
+                            out=z_bank[:, jj, :],
+                            lhsT=codes[h_q][:, k, chans].bitcast(FP8X4),
+                            lhsT_scale=planes[h_q][:, k, chans],
+                            rhs=codes[a_q][:, k, cols].bitcast(FP8X4),
+                            rhs_scale=planes[a_q][:, k, cols],
+                            start=(k == 0),
+                            stop=(k == PASSES - 1),
+                        )
+                nc.scalar.copy(out=z_groupeds[i][:, cols, 2 * jp : 2 * jp + 2], in_=z_bank[:].rearrange("p j n -> p n j"))
 
         def mix_chunks(i, chunks):
             for chunk in chunks:
@@ -322,7 +347,8 @@ def tile_soablock_pb_t_kernel(tc, attn, h_x, v_w_words, v_w_scales, v_b, x, out)
                 sort_quarter(i + SORT_AHEAD)
             if i + TRANSPOSE_AHEAD < QUARTERS:
                 quantise_quarter(i + TRANSPOSE_AHEAD)
-            mix_chunks(i, range(QUARTER // P))
+            mix_chunks(i, (0, 1))
+            mix_wide(i, (2, 3))
             if i - PROJECT_BEHIND >= 0:
                 project(groups[i - PROJECT_BEHIND])
 

from contextlib import ExitStack

import concourse.mybir as mybir
from concourse.masks import make_identity

BF16 = mybir.dt.bfloat16
F32 = mybir.dt.float32
I32 = mybir.dt.int32
U32 = mybir.dt.uint32
U8 = mybir.dt.uint8
FP8X4 = mybir.dt.float8_e4m3fn_x4
ADD = mybir.AluOpType.add

BATCH = 4
OUT_CH = 256
MID_CH = 1024
POS = 1024

P = 128
PACK = 4
K_PASS = P * PACK
PASSES = POS // K_PASS
BANK = 512

QUARTER = 512
ROW_TILES = QUARTER // P
PAIRS = ROW_TILES // 2
PAIR_ROWS = 2 * P
QUARTERS = 4 * BATCH
ROUNDS = 4 * BATCH

TRANSPOSE_AHEAD = 2
SORT_AHEAD = 3
LOAD_AHEAD = 6
WORD_ORDER = 4
PROJECT_BEHIND = 2

FLOPS = 2 * BATCH * (MID_CH * POS * POS + OUT_CH * MID_CH * POS)


def tile_soablock_pb_t_kernel(tc, attn, h_x, v_w_words, v_w_scales, v_b, x, out):
    nc = tc.nc
    x_rows = x.rearrange("b c h w -> b c (h w)")
    out_rows = out.rearrange("b c h w -> b c (h w)")

    with ExitStack() as stack:
        const = stack.enter_context(tc.tile_pool(name="const", bufs=1))
        raw_pool = stack.enter_context(tc.tile_pool(name="raw", bufs=PAIRS * (LOAD_AHEAD + 2)))
        sorted_pool = stack.enter_context(tc.tile_pool(name="sorted", bufs=3 * PAIRS))
        grouped_pool = stack.enter_context(tc.tile_pool(name="grouped", bufs=2))
        codes_pool = stack.enter_context(tc.tile_pool(name="codes", bufs=6))
        z_grouped_pool = stack.enter_context(tc.tile_pool(name="z_grouped", bufs=2))
        z_codes_pool = stack.enter_context(tc.tile_pool(name="z_codes", bufs=4))
        x_pool = stack.enter_context(tc.tile_pool(name="x", bufs=3))
        result_pool = stack.enter_context(tc.tile_pool(name="result", bufs=6))
        z_psum = stack.enter_context(tc.psum_pool(name="z_psum", bufs=3))
        wide_psum = stack.enter_context(tc.psum_pool(name="wide_psum", bufs=5))
        stack.enter_context(tc.manual_schedule())

        raws, sorteds, turned, groupeds, codes, planes = {}, {}, {}, {}, {}, {}
        z_banks, z_groupeds, z_codes, z_planes = {}, {}, {}, {}
        x_tiles, y_banks = {}, {}

        def load_pair(q, pair, step=2):
            b, half = q // 4, (q % 4) // 2
            rows = slice(half * QUARTER, (half + 1) * QUARTER)
            if q % 2 == 0:
                source = h_x[b, rows, :].rearrange("(p j) m -> p j m", j=ROW_TILES)
            else:
                source = attn[b, rows, :].rearrange("(r p) m -> p r m", p=P)
            raw = raw_pool.tile([P, 2, POS], BF16)
            for r in range(0, 2, step):
                first = 2 * pair + r
                nc.sync.dma_start(out=raw[:, r : r + step, :], in_=source[:, first : first + step, :])
            raws[q, pair] = raw

        def load_quarter(q):
            for pair in range(PAIRS):
                load_pair(q, pair)

        def load_x(b):
            x_tile = x_pool.tile([P, OUT_CH // P, POS], BF16)
            nc.sync.dma_start(out=x_tile[:], in_=x_rows[b].rearrange("(t p) n -> p t n", p=P))
            x_tiles[b] = x_tile

        def words_as_loaded(q, pair):
            words = raws[q, pair][:].bitcast(F32)
            return words.rearrange("p r (w u) -> p u r w", u=2)

        def sort_pair(q, pair):
            in_order = sorted_pool.tile([P, 2, 2, POS // 2], BF16)
            if q < WORD_ORDER:
                nc.vector.tensor_copy(out=in_order[:].bitcast(F32), in_=words_as_loaded(q, pair))
            else:
                nc.vector.tensor_copy(
                    out=in_order[:].rearrange("p u r (x s) -> p (r x) u s", s=16),
                    in_=raws[q, pair][:].rearrange("p r (x u s) -> p (r x) u s", u=2, s=16),
                )
            sorteds[q, pair] = in_order

        def sort_quarter(q):
            for pair in range(PAIRS):
                sort_pair(q, pair)

        def transpose_pair(q, pair, words):
            banks = []
            for k in range(PASSES):
                bank = wide_psum.tile([P, 2, PAIR_ROWS], F32, tag="wide")
                banks.append(bank)
            for r in range(2):
                for k in range(PASSES):
                    for u in range(2):
                        nc.tensor.transpose(
                            banks[k][:, u, r * P : (r + 1) * P],
                            words[:, u, r, k * P : (k + 1) * P],
                            ident_f32[:],
                        )
            turned[q, pair] = banks

        def empty_turned(copy, q, pair, k):
            if q not in groupeds:
                grouped = grouped_pool.tile([P, PASSES, QUARTER, PACK], BF16, align_bytes=64)
                groupeds[q] = grouped
            rows = slice(pair * PAIR_ROWS, (pair + 1) * PAIR_ROWS)
            copy(
                out=groupeds[q][:, k, rows, :].bitcast(F32),
                in_=turned[q, pair][k][:].rearrange("p u r -> p r u"),
            )

        def transpose_quarter(q, vector_bank=2):
            for pair in range(PAIRS):
                transpose_pair(q, pair, sorteds[q, pair][:].bitcast(F32))
                for k in range(PASSES):
                    number = PASSES * pair + k
                    on_vector = number == vector_bank or (number == 0 and q >= WORD_ORDER and q % 2 == 0)
                    empty_turned(nc.vector.tensor_copy if on_vector else nc.scalar.copy, q, pair, k)

        def codes_of(q):
            if q not in codes:
                code = codes_pool.tile([P, PASSES, QUARTER], U32, align_bytes=64)
                plane = codes_pool.tile([P, PASSES, QUARTER], U8, align_bytes=64)
                codes[q] = code
                planes[q] = plane
            return codes[q], planes[q]

        def quantise_pair(q, pair):
            code, plane = codes_of(q)
            rows = slice(pair * PAIR_ROWS, (pair + 1) * PAIR_ROWS)
            for k in range(PASSES):
                nc.vector.quantize_mx(
                    out=code[:, k, rows].bitcast(FP8X4),
                    scales=plane[:, k, rows],
                    in_=groupeds[q][:, k, rows, :].rearrange("p r t -> p (r t)"),
                )

        def quantise_quarter(q):
            code, plane = codes_of(q)
            nc.vector.quantize_mx(
                out=code[:].rearrange("p k r -> p (k r)").bitcast(FP8X4),
                scales=plane[:].rearrange("p k r -> p (k r)"),
                in_=groupeds[q][:].rearrange("p k r t -> p (k r t)"),
            )

        def mix(i, chunk, js):
            b, half, g = i // 4, (i % 4) // 2, i % 2
            h_q, a_q = 4 * b + 2 * g, 4 * b + 2 * half + 1
            cols = slice(chunk * P, (chunk + 1) * P)
            if js[0] == 0:
                z_bank = z_psum.tile([P, PACK, P], F32)
                z_banks[i, chunk] = z_bank
            for j in js:
                chans = slice(j * P, (j + 1) * P)
                for k in range(PASSES):
                    nc.tensor.matmul_mx(
                        out=z_banks[i, chunk][:, j, :],
                        lhsT=codes[h_q][:, k, chans].bitcast(FP8X4),
                        lhsT_scale=planes[h_q][:, k, chans],
                        rhs=codes[a_q][:, k, cols].bitcast(FP8X4),
                        rhs_scale=planes[a_q][:, k, cols],
                        start=(k == 0),
                        stop=(k == PASSES - 1),
                    )

        def empty_z(i, chunk):
            if chunk == 0:
                z_grouped = z_grouped_pool.tile([P, QUARTER, PACK], BF16, align_bytes=64)
                z_groupeds[i] = z_grouped
            cols = slice(chunk * P, (chunk + 1) * P)
            nc.scalar.copy(
                out=z_groupeds[i][:, cols, :].rearrange("p (c i) j -> p c j i", i=4),
                in_=z_banks[i, chunk][:].rearrange("p j (c i) -> p c j i", i=4),
            )

        def mix_wide(i, chunks):
            b, half, g = i // 4, (i % 4) // 2, i % 2
            h_q, a_q = 4 * b + 2 * g, 4 * b + 2 * half + 1
            cols = slice(chunks[0] * P, (chunks[0] + 2) * P)
            if chunks[0] == 0:
                z_grouped = z_grouped_pool.tile([P, QUARTER, PACK], BF16, align_bytes=64)
                z_groupeds[i] = z_grouped
            for jp in range(2):
                z_bank = z_psum.tile([P, 2, 2 * P], F32)
                for jj in range(2):
                    j = 2 * jp + jj
                    chans = slice(j * P, (j + 1) * P)
                    for k in range(PASSES):
                        nc.tensor.matmul_mx(
                            out=z_bank[:, jj, :],
                            lhsT=codes[h_q][:, k, chans].bitcast(FP8X4),
                            lhsT_scale=planes[h_q][:, k, chans],
                            rhs=codes[a_q][:, k, cols].bitcast(FP8X4),
                            rhs_scale=planes[a_q][:, k, cols],
                            start=(k == 0),
                            stop=(k == PASSES - 1),
                        )
                nc.scalar.copy(out=z_groupeds[i][:, cols, 2 * jp : 2 * jp + 2], in_=z_bank[:].rearrange("p j n -> p n j"))

        def mix_chunks(i, chunks):
            for chunk in chunks:
                mix(i, chunk, range(PACK))
                empty_z(i, chunk)

        def quantise_z(i, first, count):
            if first == 0:
                z_code = z_codes_pool.tile([P, QUARTER], U32, align_bytes=64)
                z_plane = z_codes_pool.tile([P, QUARTER], U8, align_bytes=64)
                z_codes[i] = z_code
                z_planes[i] = z_plane
            cols = slice(first, first + count)
            nc.vector.quantize_mx(
                out=z_codes[i][:, cols].bitcast(FP8X4),
                scales=z_planes[i][:, cols],
                in_=z_groupeds[i][:, cols, :].rearrange("p n j -> p (n j)"),
            )

        def project(group):
            b, half, tiles, first, count = group
            bank = wide_psum.tile([P, BANK], F32, tag="wide")
            for place, t in enumerate(tiles):
                outs = slice(t * P, (t + 1) * P)
                for g in range(PASSES):
                    i = 4 * b + 2 * half + g
                    nc.tensor.matmul_mx(
                        out=bank[:, place * count : (place + 1) * count],
                        lhsT=w_words[:, g, outs].bitcast(FP8X4),
                        lhsT_scale=w_plane[:, g, outs],
                        rhs=z_codes[i][:, first : first + count].bitcast(FP8X4),
                        rhs_scale=z_planes[i][:, first : first + count],
                        start=(g == 0),
                        stop=(g == PASSES - 1),
                    )
            y_banks[group] = bank

        def finish(group):
            b, half, tiles, first, count = group
            cols = slice(half * QUARTER + first, half * QUARTER + first + count)
            result = result_pool.tile([P, BANK], F32)
            for place, t in enumerate(tiles):
                part = slice(place * count, (place + 1) * count)
                nc.vector.scalar_tensor_tensor(
                    out=result[:, part],
                    in0=y_banks[group][:, part],
                    scalar=bias[:, t : t + 1],
                    in1=x_tiles[b][:, t, cols],
                    op0=ADD,
                    op1=ADD,
                )
            nc.sync.dma_start(
                out=out_rows[b].rearrange("(t p) n -> p t n", p=P)[:, tiles[0] : tiles[-1] + 1, cols],
                in_=result[:, 0 : len(tiles) * count].rearrange("p (t n) -> p t n", t=len(tiles)),
            )

        groups = [(n // 4, (n % 4) // 2, (n % 2,), 0, QUARTER) for n in range(4 * BATCH - 2)]
        both = tuple(range(OUT_CH // P))
        last_groups = [(BATCH - 1, 1, both, 0, 2 * P), (BATCH - 1, 1, both, 2 * P, P), (BATCH - 1, 1, both, 3 * P, P)]

        ident_f32 = const.tile([P, P], F32)
        make_identity(nc, ident_f32[:])
        ident_bf16 = const.tile([P, P], BF16)
        make_identity(nc, ident_bf16[:])

        w_words = const.tile([P, PASSES, OUT_CH], U32, align_bytes=64)
        w_plane = const.tile([P, PASSES, OUT_CH], U8, align_bytes=64)
        nc.vector.memset(w_plane[:].bitcast(I32), 0)
        bias_rows = const.tile([P, P], BF16)
        nc.vector.memset(bias_rows[:], 0.0)

        load_pair(1, 0, step=1)
        load_pair(0, 0, step=1)
        load_pair(0, 1, step=1)
        load_pair(1, 1, step=1)
        load_quarter(2)
        nc.sync.dma_start(out=bias_rows[0 : OUT_CH // P, :], in_=v_b.rearrange("(t p) -> t p", p=P))
        load_quarter(3)
        nc.sync.dma_start(
            out=w_words[:].bitcast(I32),
            in_=v_w_words.rearrange("g p o t -> p g (o t)").bitcast(I32),
        )
        for quad in range(4):
            nc.sync.dma_start(
                out=w_plane[32 * quad : 32 * quad + 4, :, :].bitcast(I32),
                in_=v_w_scales[:, 4 * quad : 4 * quad + 4, :].rearrange("g r o -> r g o").bitcast(I32),
            )
        load_x(0)
        for q in range(4, LOAD_AHEAD + 1):
            load_quarter(q)

        transpose_pair(1, 0, words_as_loaded(1, 0))
        empty_turned(nc.scalar.copy, 1, 0, 0)
        empty_turned(nc.scalar.copy, 1, 0, 1)
        quantise_pair(1, 0)
        transpose_pair(0, 0, words_as_loaded(0, 0))
        empty_turned(nc.scalar.copy, 0, 0, 0)
        empty_turned(nc.vector.tensor_copy, 0, 0, 1)
        quantise_pair(0, 0)
        transpose_pair(0, 1, words_as_loaded(0, 1))
        empty_turned(nc.scalar.copy, 0, 1, 0)
        empty_turned(nc.scalar.copy, 0, 1, 1)
        quantise_pair(0, 1)
        transpose_pair(1, 1, words_as_loaded(1, 1))
        empty_turned(nc.scalar.copy, 1, 1, 0)
        sort_pair(2, 0)
        empty_turned(nc.vector.tensor_copy, 1, 1, 1)
        mix_chunks(0, (0, 1))
        sort_pair(2, 1)
        quantise_pair(1, 1)
        transpose_quarter(2, vector_bank=1)
        sort_quarter(3)
        mix_chunks(0, (2, 3))
        quantise_quarter(2)
        bias_bank = wide_psum.tile([P, P], BF16, tag="wide")
        nc.tensor.transpose(bias_bank[:], bias_rows[:], ident_bf16[:])
        bias = const.tile([P, OUT_CH // P], F32)
        nc.vector.tensor_copy(out=bias[:], in_=bias_bank[:, 0 : OUT_CH // P])

        for i in range(1, ROUNDS - 1):
            if i + LOAD_AHEAD < QUARTERS:
                load_quarter(i + LOAD_AHEAD)
                if (i + LOAD_AHEAD) % 4 == 3:
                    load_x((i + LOAD_AHEAD) // 4)
            if i - PROJECT_BEHIND - 1 >= 0:
                finish(groups[i - PROJECT_BEHIND - 1])
            if i + TRANSPOSE_AHEAD < QUARTERS:
                transpose_quarter(i + TRANSPOSE_AHEAD)
            quantise_z(i - 1, 0, QUARTER)
            if i + SORT_AHEAD < QUARTERS:
                sort_quarter(i + SORT_AHEAD)
            if i + TRANSPOSE_AHEAD < QUARTERS:
                quantise_quarter(i + TRANSPOSE_AHEAD)
            mix_chunks(i, (0, 1))
            mix_wide(i, (2, 3))
            if i - PROJECT_BEHIND >= 0:
                project(groups[i - PROJECT_BEHIND])

        i = ROUNDS - 1
        finish(groups[-2])
        quantise_z(i - 1, 0, QUARTER)
        mix_chunks(i, (0, 1))
        quantise_z(i, 0, 2 * P)
        project(groups[-1])
        mix_chunks(i, (2,))
        quantise_z(i, 2 * P, P)
        mix_chunks(i, (3,))
        finish(groups[-1])
        quantise_z(i, 3 * P, P)
        for group in last_groups:
            project(group)
        for group in last_groups:
            finish(group)
